import numpy as np
import ml_dtypes


def mxq(x, axis, fmt="e4m3"):
    dtype, down = {"e4m3": (ml_dtypes.float8_e4m3fn, 7), "e5m2": (ml_dtypes.float8_e5m2, 14)}[fmt]
    v = np.moveaxis(np.asarray(x, np.float32).astype(ml_dtypes.bfloat16).astype(np.float64), axis, -1)
    blocks = v.reshape(v.shape[:-1] + (-1, 32))
    amax = np.abs(blocks).max(-1, keepdims=True)
    byte = np.maximum(np.where(amax > 0, np.frexp(amax)[1] - 1 + 127, 0) - down, 1)
    scale = np.exp2(byte - 127.0)
    codes = (blocks / scale).astype(np.float32).astype(dtype).astype(np.float64)
    return np.moveaxis((codes * scale).reshape(v.shape), -1, axis)


WIDE = False


def mx_kscale(k):
    if not WIDE:
        return np.ones(k)
    levels = np.array([10, -10, 5, -5, 0])
    a = np.random.permutation(np.resize(levels, k // 512 * 4)).reshape(k // 512, 4)
    idx = np.arange(k)
    return np.exp2(a[idx // 512, idx % 128 // 32])


BF16 = ml_dtypes.bfloat16


def bf(x):
    return np.asarray(x, np.float32).astype(BF16)


def f64(x):
    return np.asarray(x).astype(np.float64)


E2M1 = np.array([0.0, 0.5, 1.0, 1.5, 2.0, 3.0, 4.0, 6.0, -0.0, -0.5, -1.0, -1.5, -2.0, -3.0, -4.0, -6.0])


def pack_weight(w, fmt):
    k, n = w.shape
    w = f64(bf(w)).reshape(k // 32, 32, n)
    amax = np.abs(w).max(1)
    if fmt == "e4m3":
        byte = np.frexp(amax)[1] - 1 + 127 - 7
    else:
        mant, ex = np.frexp(amax / 6.0)
        byte = np.where(mant > 0.5, ex, ex - 1) + 127
    byte = np.clip(np.where(amax > 0, byte, 1), 1, 254)
    scaled = (w * np.exp2(127.0 - byte)[:, None, :]).reshape(k, n).astype(np.float32)
    by_word = np.ascontiguousarray(scaled.reshape(k // 512, 128, 4, n).transpose(0, 1, 3, 2))
    if fmt == "e4m3":
        words = by_word.astype(ml_dtypes.float8_e4m3fn).view(np.uint8)
    else:
        c = by_word.astype(ml_dtypes.float4_e2m1fn).view(np.uint8) & 0xF
        words = c[..., 0::2] | (c[..., 1::2] << 4)
    return np.ascontiguousarray(words), np.ascontiguousarray(byte.astype(np.uint8).reshape(k // 512, 16, n))


def unpack_weight(words, scales, fmt):
    g, p, n, _ = words.shape
    if fmt == "e4m3":
        vals = np.ascontiguousarray(words).view(ml_dtypes.float8_e4m3fn).astype(np.float64)
    else:
        nib = np.empty((g, p, n, 4), np.uint8)
        nib[..., 0::2] = words & 0xF
        nib[..., 1::2] = words >> 4
        vals = E2M1[nib]
    vals = vals * np.repeat(np.exp2(scales.astype(np.float64) - 127.0), 8, axis=1)[..., None]
    return vals.transpose(0, 1, 3, 2).reshape(g * 512, n)

def pack4(w):
    words, scales = pack_weight(w, "e2m1")
    return words.reshape(words.shape[0], 128, -1), scales


def unpack4(words, scales):
    return unpack_weight(words.reshape(words.shape[0], 128, -1, 2), scales, "e2m1")


B, L, E, H = 4, 64, 2048, 16
HD = E // H
EPS = 1e-12


def l2_normalize(t):
    n = np.sqrt(np.sum(t * t, axis=-1, keepdims=True))
    return t / np.maximum(n, EPS)


def setup_inputs():
    s = mx_kscale(E)
    x = bf(np.random.standard_normal((B, L, E)) * s)
    w = np.random.standard_normal((3 * E, E)) / np.sqrt(E) / s[None, :]
    words, scales = pack4(np.ascontiguousarray(w.T))
    b = bf(np.random.standard_normal(3 * E) * 0.3)
    return {"x": x, "W_words": words, "W_scales": scales, "b": b}


def reference(x, W_words, W_scales, b):
    y = (mxq(f64(x), 2, "e4m3") @ unpack4(W_words, W_scales)) + f64(b)
    y = y.reshape(B, L, H, 3, HD)
    q = np.transpose(y[..., 0, :], (0, 2, 1, 3))
    k = np.transpose(y[..., 1, :], (0, 2, 1, 3))
    v = np.transpose(y[..., 2, :], (0, 2, 1, 3))
    return l2_normalize(q), l2_normalize(k), v

@@ -1,0 +1,186 @@
+from contextlib import ExitStack
+
+import concourse.mybir as mybir
+from concourse.masks import make_identity
+
+F32 = mybir.dt.float32
+BF16 = mybir.dt.bfloat16
+I32 = mybir.dt.int32
+U32 = mybir.dt.uint32
+U8 = mybir.dt.uint8
+FP8X4 = mybir.dt.float8_e4m3fn_x4
+FP4X4 = mybir.dt.float4_e2m1fn_x4
+ADD = mybir.AluOpType.add
+MULT = mybir.AluOpType.mult
+SQUARE = mybir.ActivationFunctionType.Square
+
+P = 128
+BATCH, POSITIONS, CHANNELS, HEADS = 4, 64, 2048, 16
+HEAD_DIM = CHANNELS // HEADS
+KINDS = 3
+COLUMNS = KINDS * CHANNELS
+SIDES = 2
+PAIRS = POSITIONS // SIDES
+K_PASS = 4 * P
+GROUPS = CHANNELS // K_PASS
+BANK = 512
+UNIT_HEADS = 4
+UNIT = UNIT_HEADS * KINDS * HEAD_DIM
+UNITS = COLUMNS // UNIT
+UNIT_BANKS = UNIT // BANK
+BANK_VECTORS = BANK // HEAD_DIM
+EPS = 1e-12
+
+FLOPS = 2 * BATCH * POSITIONS * CHANNELS * COLUMNS
+
+
+def tile_selfattention_pa_kernel(tc, x, W_words, W_scales, b, out_0, out_1, out_2):
+    nc = tc.nc
+    outs = (out_0, out_1, out_2)
+    with ExitStack() as ctx:
+        keep = ctx.enter_context(tc.tile_pool(name="keep", bufs=1))
+        results = ctx.enter_context(tc.tile_pool(name="results", bufs=UNITS))
+        scratch = ctx.enter_context(tc.tile_pool(name="scratch", bufs=2))
+        psum = ctx.enter_context(tc.psum_pool(name="psum", bufs=8))
+
+        x_sb = keep.tile([P, SIDES, CHANNELS], BF16)
+        for batch in range(BATCH):
+            nc.sync.dma_start(
+                out=x_sb[batch:P:BATCH],
+                in_=x[batch].rearrange("(pair side) e -> pair side e", side=SIDES),
+            )
+
+        bias_rows = keep.tile([P, BANK], BF16)
+        nc.vector.memset(bias_rows[:].bitcast(I32), 0)
+        nc.scalar.dma_start(
+            out=bias_rows[0 : COLUMNS // BANK, :], in_=b.rearrange("(c n) -> c n", n=BANK)
+        )
+
+        words_dram = W_words.bitcast(I32)
+        scales_dram = W_scales.bitcast(I32)
+        w_words = []
+        w_scales = []
+        for unit in range(UNITS):
+            plane = keep.tile([P, GROUPS, UNIT], U8, name="w_scales%d" % unit, align_bytes=64)
+            nc.vector.memset(plane[:].bitcast(I32), 0)
+            scale_cols = slice(unit * UNIT // 4, (unit + 1) * UNIT // 4)
+            for q in range(8):
+                live_row = 32 * (q // 4) + q % 4
+                nc.sync.dma_start(
+                    out=plane[live_row:P:64].bitcast(I32),
+                    in_=scales_dram[:, q:16:8, scale_cols].rearrange("g q n -> q g n"),
+                )
+            words = keep.tile([P, GROUPS, 2 * UNIT], U8, name="w_words%d" % unit, align_bytes=64)
+            word_cols = slice(unit * UNIT // 2, (unit + 1) * UNIT // 2)
+            nc.sync.dma_start(
+                out=words[:].bitcast(I32),
+                in_=words_dram[:, :, word_cols].rearrange("g p n -> p g n"),
+            )
+            w_words.append(words)
+            w_scales.append(plane)
+
+        ident_bf16 = keep.tile([P, P], BF16)
+        make_identity(nc, ident_bf16[:])
+        bias_all = keep.tile([P, COLUMNS], BF16)
+        for half in range(COLUMNS // (2 * BANK)):
+            bias_ps = psum.tile([P, 2 * BANK], BF16, tag="bank")
+            for i in range(2):
+                c = 2 * half + i
+                nc.tensor.matmul(
+                    out=bias_ps[:, i * BANK : (i + 1) * BANK],
+                    lhsT=ident_bf16[:, c : c + 1].to_broadcast([P, P]),
+                    rhs=bias_rows[:],
+                    start=True,
+                    stop=True,
+                )
+            nc.scalar.copy(out=bias_all[:, 2 * half * BANK : 2 * (half + 1) * BANK], in_=bias_ps[:])
+
+        ident_f32 = keep.tile([P, P], F32)
+        make_identity(nc, ident_f32[:])
+        x_pairs = x_sb[:].bitcast(F32).rearrange("r s (g p u) -> r s g p u", g=GROUPS, u=2)
+        x_codes = []
+        x_scales = []
+        for side in range(SIDES):
+            grouped = keep.tile([P, 4 * GROUPS * P], BF16, name="grouped%d" % side, align_bytes=64)
+            grouped_pairs = grouped[:].bitcast(F32).rearrange("p (g r u) -> p g r u", g=GROUPS, u=2)
+            for g0 in range(0, GROUPS, 2):
+                xt = psum.tile([P, 2, 2, P], F32, tag="bank")
+                for i in range(2):
+                    for u in range(2):
+                        nc.tensor.transpose(
+                            xt[:, i, u, :], x_pairs[:, side, g0 + i, :, u], ident_f32[:]
+                        )
+                nc.vector.tensor_copy(
+                    out=grouped_pairs[:, g0 : g0 + 2],
+                    in_=xt[:].rearrange("p g u r -> p g r u"),
+                )
+            codes = keep.tile([P, GROUPS * P], U32, name="x_codes%d" % side, align_bytes=64)
+            plane = keep.tile([P, GROUPS * P], U8, name="x_scales%d" % side, align_bytes=64)
+            nc.vector.quantize_mx(out=codes[:].bitcast(FP8X4), scales=plane[:], in_=grouped[:])
+            x_codes.append(codes)
+            x_scales.append(plane)
+
+        for unit in range(UNITS):
+            y = results.tile([P, UNIT_HEADS, KINDS, SIDES, HEAD_DIM], F32)
+            y_vectors = y[:].rearrange("p h t s d -> p (h t) s d")
+            for bank in range(UNIT_BANKS):
+                for side in range(SIDES):
+                    acc = psum.tile([P, BANK], F32, tag="bank")
+                    for g in range(GROUPS):
+                        tokens = slice(g * P, (g + 1) * P)
+                        nc.tensor.matmul_mx(
+                            out=acc[:],
+                            lhsT=x_codes[side][:, tokens].bitcast(FP8X4),
+                            lhsT_scale=x_scales[side][:, tokens],
+                            rhs=w_words[unit][:, g, 2 * bank * BANK : 2 * (bank + 1) * BANK].bitcast(FP4X4),
+                            rhs_scale=w_scales[unit][:, g, bank * BANK : (bank + 1) * BANK],
+                            start=(g == 0),
+                            stop=(g == GROUPS - 1),
+                        )
+                    first_col = unit * UNIT + bank * BANK
+                    nc.vector.tensor_tensor(
+                        out=y_vectors[:, bank * BANK_VECTORS : (bank + 1) * BANK_VECTORS, side, :],
+                        in0=acc[:].rearrange("p (v d) -> p v d", d=HEAD_DIM),
+                        in1=bias_all[:, first_col : first_col + BANK].rearrange(
+                            "p (v d) -> p v d", d=HEAD_DIM
+                        ),
+                        op=ADD,
+                    )
+
+            def store(kind):
+                heads = slice(unit * UNIT_HEADS, (unit + 1) * UNIT_HEADS)
+                for batch in range(BATCH):
+                    nc.sync.dma_start(
+                        out=outs[kind][batch, heads].rearrange(
+                            "h (pair side) d -> pair h (side d)", side=SIDES
+                        ),
+                        in_=y[batch:P:BATCH, :, kind].rearrange("p h s d -> p h (s d)"),
+                    )
+
+            store(2)
+
+            normed = 2 * SIDES
+            qk = y[:, :, 0:2].rearrange("p h t s d -> p h (t s) d")
+            squares = scratch.tile([P, UNIT_HEADS, normed, HEAD_DIM], F32)
+            sumsq = scratch.tile([P, UNIT_HEADS, normed], F32)
+            for h in range(UNIT_HEADS):
+                for v in range(normed):
+                    nc.scalar.activation(
+                        out=squares[:, h, v, :],
+                        in_=qk[:, h, v, :],
+                        func=SQUARE,
+                        accum_out=sumsq[:, h, v : v + 1],
+                    )
+            norm = scratch.tile([P, UNIT_HEADS, normed], F32)
+            inv_norm = scratch.tile([P, UNIT_HEADS, normed], F32)
+            nc.vector.tensor_scalar_max(out=sumsq[:], in0=sumsq[:], scalar1=EPS * EPS)
+            nc.scalar.sqrt(out=norm[:], in_=sumsq[:])
+            nc.vector.reciprocal(out=inv_norm[:], in_=norm[:])
+            nc.vector.tensor_tensor(
+                out=qk,
+                in0=qk,
+                in1=inv_norm[:].unsqueeze(3).to_broadcast([P, UNIT_HEADS, normed, HEAD_DIM]),
+                op=MULT,
+            )
+            store(0)
+            store(1)

@@ -13,6 +13,7 @@ FP4X4 = mybir.dt.float4_e2m1fn_x4
 ADD = mybir.AluOpType.add
 MULT = mybir.AluOpType.mult
 SQUARE = mybir.ActivationFunctionType.Square
+RSQRT = mybir.ActivationFunctionType.Abs_reciprocal_sqrt
 
 P = 128
 BATCH, POSITIONS, CHANNELS, HEADS = 4, 64, 2048, 16
@@ -29,6 +30,11 @@ UNIT = UNIT_HEADS * KINDS * HEAD_DIM
 UNITS = COLUMNS // UNIT
 UNIT_BANKS = UNIT // BANK
 BANK_VECTORS = BANK // HEAD_DIM
+HALF_HEADS = UNIT_HEADS // 2
+NORMED = 2 * SIDES
+BIAS_TILE = 2 * BANK
+BIAS_TILES = COLUMNS // BIAS_TILE
+BIAS_AHEAD = 2
 EPS = 1e-12
 
 FLOPS = 2 * BATCH * POSITIONS * CHANNELS * COLUMNS
@@ -38,6 +44,7 @@ def tile_selfattention_pa_kernel(tc, x, W_words, W_scales, b, out_0, out_1, out_
     nc = tc.nc
     outs = (out_0, out_1, out_2)
     with ExitStack() as ctx:
+        ctx.enter_context(tc.manual_schedule())
         keep = ctx.enter_context(tc.tile_pool(name="keep", bufs=1))
         results = ctx.enter_context(tc.tile_pool(name="results", bufs=UNITS))
         scratch = ctx.enter_context(tc.tile_pool(name="scratch", bufs=2))
@@ -71,32 +78,40 @@ def tile_selfattention_pa_kernel(tc, x, W_words, W_scales, b, out_0, out_1, out_
                     in_=scales_dram[:, q:16:8, scale_cols].rearrange("g q n -> q g n"),
                 )
             words = keep.tile([P, GROUPS, 2 * UNIT], U8, name="w_words%d" % unit, align_bytes=64)
-            word_cols = slice(unit * UNIT // 2, (unit + 1) * UNIT // 2)
-            nc.sync.dma_start(
-                out=words[:].bitcast(I32),
-                in_=words_dram[:, :, word_cols].rearrange("g p n -> p g n"),
-            )
+            pieces = UNIT_BANKS if unit == 0 else 1
+            piece = UNIT // 2 // pieces
+            for i in range(pieces):
+                nc.sync.dma_start(
+                    out=words[:].bitcast(I32)[:, :, i * piece : (i + 1) * piece],
+                    in_=words_dram[
+                        :, :, unit * UNIT // 2 + i * piece : unit * UNIT // 2 + (i + 1) * piece
+                    ].rearrange("g p n -> p g n"),
+                )
             w_words.append(words)
             w_scales.append(plane)
 
         ident_bf16 = keep.tile([P, P], BF16)
         make_identity(nc, ident_bf16[:])
+        ident_f32 = keep.tile([P, P], F32)
+        make_identity(nc, ident_f32[:])
         bias_all = keep.tile([P, COLUMNS], BF16)
-        for half in range(COLUMNS // (2 * BANK)):
-            bias_ps = psum.tile([P, 2 * BANK], BF16, tag="bank")
-            for i in range(2):
-                c = 2 * half + i
+
+        def spread_bias(i):
+            bias_ps = psum.tile([P, BIAS_TILE], BF16, tag="bank")
+            for j in range(BIAS_TILE // BANK):
+                c = i * (BIAS_TILE // BANK) + j
                 nc.tensor.matmul(
-                    out=bias_ps[:, i * BANK : (i + 1) * BANK],
+                    out=bias_ps[:, j * BANK : (j + 1) * BANK],
                     lhsT=ident_bf16[:, c : c + 1].to_broadcast([P, P]),
                     rhs=bias_rows[:],
                     start=True,
                     stop=True,
                 )
-            nc.scalar.copy(out=bias_all[:, 2 * half * BANK : 2 * (half + 1) * BANK], in_=bias_ps[:])
+            nc.scalar.copy(out=bias_all[:, i * BIAS_TILE : (i + 1) * BIAS_TILE], in_=bias_ps[:])
 
-        ident_f32 = keep.tile([P, P], F32)
-        make_identity(nc, ident_f32[:])
+        for i in range(BIAS_AHEAD):
+            spread_bias(i)
+
         x_pairs = x_sb[:].bitcast(F32).rearrange("r s (g p u) -> r s g p u", g=GROUPS, u=2)
         x_codes = []
         x_scales = []
@@ -110,9 +125,9 @@ def tile_selfattention_pa_kernel(tc, x, W_words, W_scales, b, out_0, out_1, out_
                         nc.tensor.transpose(
                             xt[:, i, u, :], x_pairs[:, side, g0 + i, :, u], ident_f32[:]
                         )
-                nc.vector.tensor_copy(
-                    out=grouped_pairs[:, g0 : g0 + 2],
-                    in_=xt[:].rearrange("p g u r -> p g r u"),
+                copy_out = nc.vector.tensor_copy if g0 == 0 else nc.scalar.copy
+                copy_out(
+                    out=grouped_pairs[:, g0 : g0 + 2], in_=xt[:].rearrange("p g u r -> p g r u")
                 )
             codes = keep.tile([P, GROUPS * P], U32, name="x_codes%d" % side, align_bytes=64)
             plane = keep.tile([P, GROUPS * P], U8, name="x_scales%d" % side, align_bytes=64)
@@ -120,67 +135,78 @@ def tile_selfattention_pa_kernel(tc, x, W_words, W_scales, b, out_0, out_1, out_
             x_codes.append(codes)
             x_scales.append(plane)
 
-        for unit in range(UNITS):
-            y = results.tile([P, UNIT_HEADS, KINDS, SIDES, HEAD_DIM], F32)
+        def project(unit, bank, y):
             y_vectors = y[:].rearrange("p h t s d -> p (h t) s d")
-            for bank in range(UNIT_BANKS):
-                for side in range(SIDES):
-                    acc = psum.tile([P, BANK], F32, tag="bank")
-                    for g in range(GROUPS):
-                        tokens = slice(g * P, (g + 1) * P)
-                        nc.tensor.matmul_mx(
-                            out=acc[:],
-                            lhsT=x_codes[side][:, tokens].bitcast(FP8X4),
-                            lhsT_scale=x_scales[side][:, tokens],
-                            rhs=w_words[unit][:, g, 2 * bank * BANK : 2 * (bank + 1) * BANK].bitcast(FP4X4),
-                            rhs_scale=w_scales[unit][:, g, bank * BANK : (bank + 1) * BANK],
-                            start=(g == 0),
-                            stop=(g == GROUPS - 1),
-                        )
-                    first_col = unit * UNIT + bank * BANK
-                    nc.vector.tensor_tensor(
-                        out=y_vectors[:, bank * BANK_VECTORS : (bank + 1) * BANK_VECTORS, side, :],
-                        in0=acc[:].rearrange("p (v d) -> p v d", d=HEAD_DIM),
-                        in1=bias_all[:, first_col : first_col + BANK].rearrange(
-                            "p (v d) -> p v d", d=HEAD_DIM
-                        ),
-                        op=ADD,
+            first_col = unit * UNIT + bank * BANK
+            for side in range(SIDES):
+                acc = psum.tile([P, BANK], F32, tag="bank")
+                for g in range(GROUPS):
+                    tokens = slice(g * P, (g + 1) * P)
+                    nc.tensor.matmul_mx(
+                        out=acc[:],
+                        lhsT=x_codes[side][:, tokens].bitcast(FP8X4),
+                        lhsT_scale=x_scales[side][:, tokens],
+                        rhs=w_words[unit][:, g, 2 * bank * BANK : 2 * (bank + 1) * BANK].bitcast(FP4X4),
+                        rhs_scale=w_scales[unit][:, g, bank * BANK : (bank + 1) * BANK],
+                        start=(g == 0),
+                        stop=(g == GROUPS - 1),
                     )
+                nc.vector.tensor_tensor(
+                    out=y_vectors[:, bank * BANK_VECTORS : (bank + 1) * BANK_VECTORS, side, :],
+                    in0=acc[:].rearrange("p (v d) -> p v d", d=HEAD_DIM),
+                    in1=bias_all[:, first_col : first_col + BANK].rearrange(
+                        "p (v d) -> p v d", d=HEAD_DIM
+                    ),
+                    op=ADD,
+                )
 
-            def store(kind):
-                heads = slice(unit * UNIT_HEADS, (unit + 1) * UNIT_HEADS)
-                for batch in range(BATCH):
-                    nc.sync.dma_start(
-                        out=outs[kind][batch, heads].rearrange(
-                            "h (pair side) d -> pair h (side d)", side=SIDES
-                        ),
-                        in_=y[batch:P:BATCH, :, kind].rearrange("p h s d -> p h (s d)"),
-                    )
+        def store(unit, half, kind, y):
+            h_unit = half * HALF_HEADS
+            h_all = unit * UNIT_HEADS + h_unit
+            for batch in range(BATCH):
+                nc.sync.dma_start(
+                    out=outs[kind][batch, h_all : h_all + HALF_HEADS].rearrange(
+                        "h (pair side) d -> pair h (side d)", side=SIDES
+                    ),
+                    in_=y[batch:P:BATCH, h_unit : h_unit + HALF_HEADS, kind].rearrange(
+                        "p h s d -> p h (s d)"
+                    ),
+                )
 
-            store(2)
-
-            normed = 2 * SIDES
-            qk = y[:, :, 0:2].rearrange("p h t s d -> p h (t s) d")
-            squares = scratch.tile([P, UNIT_HEADS, normed, HEAD_DIM], F32)
-            sumsq = scratch.tile([P, UNIT_HEADS, normed], F32)
-            for h in range(UNIT_HEADS):
-                for v in range(normed):
+        def finish(unit, half, y):
+            store(unit, half, 2, y)
+            qk = y[:, half * HALF_HEADS : (half + 1) * HALF_HEADS, 0:2].rearrange(
+                "p h t s d -> p h (t s) d"
+            )
+            squares = scratch.tile([P, HALF_HEADS, NORMED, HEAD_DIM], F32)
+            sumsq = scratch.tile([P, HALF_HEADS, NORMED], F32)
+            for h in range(HALF_HEADS):
+                for v in range(NORMED):
                     nc.scalar.activation(
                         out=squares[:, h, v, :],
                         in_=qk[:, h, v, :],
                         func=SQUARE,
                         accum_out=sumsq[:, h, v : v + 1],
                     )
-            norm = scratch.tile([P, UNIT_HEADS, normed], F32)
-            inv_norm = scratch.tile([P, UNIT_HEADS, normed], F32)
-            nc.vector.tensor_scalar_max(out=sumsq[:], in0=sumsq[:], scalar1=EPS * EPS)
-            nc.scalar.sqrt(out=norm[:], in_=sumsq[:])
-            nc.vector.reciprocal(out=inv_norm[:], in_=norm[:])
-            nc.vector.tensor_tensor(
+            inv_norm = scratch.tile([P, HALF_HEADS, NORMED], F32)
+            nc.scalar.activation(out=inv_norm[:], in_=sumsq[:], func=RSQRT)
+            nc.gpsimd.tensor_scalar_min(out=inv_norm[:], in0=inv_norm[:], scalar1=1.0 / EPS)
+            nc.gpsimd.tensor_tensor(
                 out=qk,
                 in0=qk,
-                in1=inv_norm[:].unsqueeze(3).to_broadcast([P, UNIT_HEADS, normed, HEAD_DIM]),
+                in1=inv_norm[:].unsqueeze(3).to_broadcast([P, HALF_HEADS, NORMED, HEAD_DIM]),
                 op=MULT,
             )
-            store(0)
-            store(1)
+            store(unit, half, 0, y)
+            store(unit, half, 1, y)
+
+        for unit in range(UNITS):
+            y = results.tile([P, UNIT_HEADS, KINDS, SIDES, HEAD_DIM], F32)
+            for bank in range(UNIT_BANKS):
+                banks_done = unit * UNIT_BANKS + bank
+                next_bias = banks_done // 2 + BIAS_AHEAD
+                if banks_done % 2 == 0 and next_bias < BIAS_TILES:
+                    spread_bias(next_bias)
+                project(unit, bank, y)
+                if bank >= 1:
+                    finish(unit, bank - 1, y)

@@ -31,7 +31,6 @@ UNITS = COLUMNS // UNIT
 UNIT_BANKS = UNIT // BANK
 BANK_VECTORS = BANK // HEAD_DIM
 HALF_HEADS = UNIT_HEADS // 2
-NORMED = 2 * SIDES
 BIAS_TILE = 2 * BANK
 BIAS_TILES = COLUMNS // BIAS_TILE
 BIAS_AHEAD = 2
@@ -160,46 +159,55 @@ def tile_selfattention_pa_kernel(tc, x, W_words, W_scales, b, out_0, out_1, out_
                     op=ADD,
                 )
 
-        def store(unit, half, kind, y):
-            h_unit = half * HALF_HEADS
+        def store(unit, h_unit, heads, y):
             h_all = unit * UNIT_HEADS + h_unit
-            for batch in range(BATCH):
-                nc.sync.dma_start(
-                    out=outs[kind][batch, h_all : h_all + HALF_HEADS].rearrange(
-                        "h (pair side) d -> pair h (side d)", side=SIDES
-                    ),
-                    in_=y[batch:P:BATCH, h_unit : h_unit + HALF_HEADS, kind].rearrange(
-                        "p h s d -> p h (s d)"
-                    ),
+            for kind in (2, 0, 1):
+                for batch in range(BATCH):
+                    nc.sync.dma_start(
+                        out=outs[kind][batch, h_all : h_all + heads].rearrange(
+                            "h (pair side) d -> pair h (side d)", side=SIDES
+                        ),
+                        in_=y[batch:P:BATCH, h_unit : h_unit + heads, kind].rearrange(
+                            "p h s d -> p h (s d)"
+                        ),
+                    )
+
+        def inverse_norms(half, y):
+            squares = scratch.tile([P, HALF_HEADS, 2, SIDES, HEAD_DIM], F32)
+            sumsq = scratch.tile([P, HALF_HEADS, 2, SIDES], F32)
+            for h in range(HALF_HEADS):
+                for kind in range(2):
+                    for side in range(SIDES):
+                        nc.scalar.activation(
+                            out=squares[:, h, kind, side, :],
+                            in_=y[:, half * HALF_HEADS + h, kind, side, :],
+                            func=SQUARE,
+                            accum_out=sumsq[:, h, kind, side : side + 1],
+                        )
+            rsqrt = scratch.tile([P, HALF_HEADS, 2, SIDES], F32)
+            nc.scalar.activation(out=rsqrt[:], in_=sumsq[:], func=RSQRT)
+            return rsqrt
+
+        def normalise(half, y, rsqrt):
+            heads = slice(half * HALF_HEADS, (half + 1) * HALF_HEADS)
+            for kind, engine in ((0, nc.vector), (1, nc.gpsimd)):
+                inv_norm = scratch.tile([P, HALF_HEADS, SIDES], F32, name="inv_norm%d" % kind)
+                engine.tensor_scalar_min(out=inv_norm[:], in0=rsqrt[:, :, kind, :], scalar1=1.0 / EPS)
+                engine.tensor_tensor(
+                    out=y[:, heads, kind],
+                    in0=y[:, heads, kind],
+                    in1=inv_norm[:].unsqueeze(3).to_broadcast([P, HALF_HEADS, SIDES, HEAD_DIM]),
+                    op=MULT,
                 )
 
-        def finish(unit, half, y):
-            store(unit, half, 2, y)
-            qk = y[:, half * HALF_HEADS : (half + 1) * HALF_HEADS, 0:2].rearrange(
-                "p h t s d -> p h (t s) d"
-            )
-            squares = scratch.tile([P, HALF_HEADS, NORMED, HEAD_DIM], F32)
-            sumsq = scratch.tile([P, HALF_HEADS, NORMED], F32)
-            for h in range(HALF_HEADS):
-                for v in range(NORMED):
-                    nc.scalar.activation(
-                        out=squares[:, h, v, :],
-                        in_=qk[:, h, v, :],
-                        func=SQUARE,
-                        accum_out=sumsq[:, h, v : v + 1],
-                    )
-            inv_norm = scratch.tile([P, HALF_HEADS, NORMED], F32)
-            nc.scalar.activation(out=inv_norm[:], in_=sumsq[:], func=RSQRT)
-            nc.gpsimd.tensor_scalar_min(out=inv_norm[:], in0=inv_norm[:], scalar1=1.0 / EPS)
-            nc.gpsimd.tensor_tensor(
-                out=qk,
-                in0=qk,
-                in1=inv_norm[:].unsqueeze(3).to_broadcast([P, HALF_HEADS, NORMED, HEAD_DIM]),
-                op=MULT,
-            )
-            store(unit, half, 0, y)
-            store(unit, half, 1, y)
+        def finish(unit, half, y, rsqrt):
+            normalise(half, y, rsqrt)
+            heads_a_store = HALF_HEADS if unit == UNITS - 1 else UNIT_HEADS
+            heads_done = (half + 1) * HALF_HEADS
+            if heads_done % heads_a_store == 0:
+                store(unit, heads_done - heads_a_store, heads_a_store, y)
 
+        begun = []
         for unit in range(UNITS):
             y = results.tile([P, UNIT_HEADS, KINDS, SIDES, HEAD_DIM], F32)
             for bank in range(UNIT_BANKS):
@@ -208,5 +216,10 @@ def tile_selfattention_pa_kernel(tc, x, W_words, W_scales, b, out_0, out_1, out_
                 if banks_done % 2 == 0 and next_bias < BIAS_TILES:
                     spread_bias(next_bias)
                 project(unit, bank, y)
+                for job in begun:
+                    finish(*job)
+                begun = []
                 if bank >= 1:
-                    finish(unit, bank - 1, y)
+                    begun = [(unit, bank - 1, y, inverse_norms(bank - 1, y))]
+        for job in begun:
+            finish(*job)

@@ -12,6 +12,7 @@ FP8X4 = mybir.dt.float8_e4m3fn_x4
 FP4X4 = mybir.dt.float4_e2m1fn_x4
 ADD = mybir.AluOpType.add
 MULT = mybir.AluOpType.mult
+MIN = mybir.AluOpType.min
 SQUARE = mybir.ActivationFunctionType.Square
 RSQRT = mybir.ActivationFunctionType.Abs_reciprocal_sqrt
 
@@ -159,18 +160,21 @@ def tile_selfattention_pa_kernel(tc, x, W_words, W_scales, b, out_0, out_1, out_
                     op=ADD,
                 )
 
-        def store(unit, h_unit, heads, y):
+        def store_kind(unit, h_unit, heads, kind, y):
             h_all = unit * UNIT_HEADS + h_unit
+            for batch in range(BATCH):
+                nc.sync.dma_start(
+                    out=outs[kind][batch, h_all : h_all + heads].rearrange(
+                        "h (pair side) d -> pair h (side d)", side=SIDES
+                    ),
+                    in_=y[batch:P:BATCH, h_unit : h_unit + heads, kind].rearrange(
+                        "p h s d -> p h (s d)"
+                    ),
+                )
+
+        def store(unit, h_unit, heads, y):
             for kind in (2, 0, 1):
-                for batch in range(BATCH):
-                    nc.sync.dma_start(
-                        out=outs[kind][batch, h_all : h_all + heads].rearrange(
-                            "h (pair side) d -> pair h (side d)", side=SIDES
-                        ),
-                        in_=y[batch:P:BATCH, h_unit : h_unit + heads, kind].rearrange(
-                            "p h s d -> p h (s d)"
-                        ),
-                    )
+                store_kind(unit, h_unit, heads, kind, y)
 
         def inverse_norms(half, y):
             squares = scratch.tile([P, HALF_HEADS, 2, SIDES, HEAD_DIM], F32)
@@ -202,13 +206,63 @@ def tile_selfattention_pa_kernel(tc, x, W_words, W_scales, b, out_0, out_1, out_
 
         def finish(unit, half, y, rsqrt):
             normalise(half, y, rsqrt)
-            heads_a_store = HALF_HEADS if unit == UNITS - 1 else UNIT_HEADS
-            heads_done = (half + 1) * HALF_HEADS
-            if heads_done % heads_a_store == 0:
-                store(unit, heads_done - heads_a_store, heads_a_store, y)
+            if half == 1:
+                store(unit, 0, UNIT_HEADS, y)
+
+        def project_piece(unit, kind, half, y):
+            heads = slice(half * HALF_HEADS, (half + 1) * HALF_HEADS)
+            bias_unit = bias_all[:, unit * UNIT : (unit + 1) * UNIT].rearrange(
+                "p (h t d) -> p h t d", t=KINDS, d=HEAD_DIM
+            )
+            for side in range(SIDES):
+                acc = psum.tile([P, HALF_HEADS, HEAD_DIM], F32, tag="bank")
+                for h in range(HALF_HEADS):
+                    col = ((half * HALF_HEADS + h) * KINDS + kind) * HEAD_DIM
+                    for g in range(GROUPS):
+                        tokens = slice(g * P, (g + 1) * P)
+                        nc.tensor.matmul_mx(
+                            out=acc[:, h, :],
+                            lhsT=x_codes[side][:, tokens].bitcast(FP8X4),
+                            lhsT_scale=x_scales[side][:, tokens],
+                            rhs=w_words[unit][:, g, 2 * col : 2 * (col + HEAD_DIM)].bitcast(FP4X4),
+                            rhs_scale=w_scales[unit][:, g, col : col + HEAD_DIM],
+                            start=(g == 0),
+                            stop=(g == GROUPS - 1),
+                        )
+                nc.vector.tensor_tensor(
+                    out=y[:, heads, kind, side, :], in0=acc[:], in1=bias_unit[:, heads, kind, :], op=ADD
+                )
+
+        def piece_norms(kind, half, y):
+            squares_p = scratch.tile([P, SIDES, HALF_HEADS, HEAD_DIM], F32)
+            sumsq_p = scratch.tile([P, HALF_HEADS, SIDES], F32)
+            for side in range(SIDES):
+                for h in range(HALF_HEADS):
+                    nc.scalar.activation(
+                        out=squares_p[:, side, h, :],
+                        in_=y[:, half * HALF_HEADS + h, kind, side, :],
+                        func=SQUARE,
+                        accum_out=sumsq_p[:, h, side : side + 1],
+                    )
+            rsqrt_p = scratch.tile([P, HALF_HEADS, SIDES], F32)
+            nc.scalar.activation(out=rsqrt_p[:], in_=sumsq_p[:], func=RSQRT)
+            return rsqrt_p
+
+        def finish_piece(unit, kind, half, y, rsqrt_p):
+            heads = slice(half * HALF_HEADS, (half + 1) * HALF_HEADS)
+            nc.vector.scalar_tensor_tensor(
+                out=y[:, heads, kind],
+                in0=rsqrt_p[:].unsqueeze(3).to_broadcast([P, HALF_HEADS, SIDES, HEAD_DIM]),
+                scalar=1.0 / EPS,
+                in1=y[:, heads, kind],
+                op0=MIN,
+                op1=MULT,
+            )
+            if half == 1:
+                store_kind(unit, 0, UNIT_HEADS, kind, y)
 
         begun = []
-        for unit in range(UNITS):
+        for unit in range(UNITS - 1):
             y = results.tile([P, UNIT_HEADS, KINDS, SIDES, HEAD_DIM], F32)
             for bank in range(UNIT_BANKS):
                 banks_done = unit * UNIT_BANKS + bank
@@ -221,5 +275,19 @@ def tile_selfattention_pa_kernel(tc, x, W_words, W_scales, b, out_0, out_1, out_
                 begun = []
                 if bank >= 1:
                     begun = [(unit, bank - 1, y, inverse_norms(bank - 1, y))]
-        for job in begun:
-            finish(*job)
+
+        unit = UNITS - 1
+        y_last = results.tile([P, UNIT_HEADS, KINDS, SIDES, HEAD_DIM], F32, name="y")
+        pieces_begun = []
+        for kind in range(KINDS):
+            for half in range(2):
+                project_piece(unit, kind, half, y_last)
+                for job in begun:
+                    finish(*job)
+                begun = []
+                for job in pieces_begun:
+                    finish_piece(*job)
+                pieces_begun = []
+                if kind < 2:
+                    pieces_begun = [(unit, kind, half, y_last, piece_norms(kind, half, y_last))]
+        store_kind(unit, 0, UNIT_HEADS, 2, y_last)

@@ -32,9 +32,10 @@ UNITS = COLUMNS // UNIT
 UNIT_BANKS = UNIT // BANK
 BANK_VECTORS = BANK // HEAD_DIM
 HALF_HEADS = UNIT_HEADS // 2
-BIAS_TILE = 2 * BANK
+HEAD_COLUMNS = KINDS * HEAD_DIM
+BIAS_TILE_HEADS = 2
+BIAS_TILE = BIAS_TILE_HEADS * HEAD_COLUMNS
 BIAS_TILES = COLUMNS // BIAS_TILE
-BIAS_AHEAD = 2
 EPS = 1e-12
 
 FLOPS = 2 * BATCH * POSITIONS * CHANNELS * COLUMNS
@@ -50,18 +51,18 @@ def tile_selfattention_pa_kernel(tc, x, W_words, W_scales, b, out_0, out_1, out_
         scratch = ctx.enter_context(tc.tile_pool(name="scratch", bufs=2))
         psum = ctx.enter_context(tc.psum_pool(name="psum", bufs=8))
 
+        bias_rows = keep.tile([P, HEAD_COLUMNS], BF16)
+        nc.gpsimd.memset(bias_rows[:], 0.0)
+        nc.sync.dma_start(
+            out=bias_rows[0:HEADS, :], in_=b.rearrange("(c n) -> c n", n=HEAD_COLUMNS)
+        )
+
         x_sb = keep.tile([P, SIDES, CHANNELS], BF16)
         for batch in range(BATCH):
             nc.sync.dma_start(
                 out=x_sb[batch:P:BATCH],
                 in_=x[batch].rearrange("(pair side) e -> pair side e", side=SIDES),
             )
-
-        bias_rows = keep.tile([P, BANK], BF16)
-        nc.vector.memset(bias_rows[:].bitcast(I32), 0)
-        nc.scalar.dma_start(
-            out=bias_rows[0 : COLUMNS // BANK, :], in_=b.rearrange("(c n) -> c n", n=BANK)
-        )
 
         words_dram = W_words.bitcast(I32)
         scales_dram = W_scales.bitcast(I32)
@@ -97,19 +98,23 @@ def tile_selfattention_pa_kernel(tc, x, W_words, W_scales, b, out_0, out_1, out_
         bias_all = keep.tile([P, COLUMNS], BF16)
 
         def spread_bias(i):
-            bias_ps = psum.tile([P, BIAS_TILE], BF16, tag="bank")
-            for j in range(BIAS_TILE // BANK):
-                c = i * (BIAS_TILE // BANK) + j
+            bias_ps = psum.tile([P, BIAS_TILE_HEADS, HEAD_COLUMNS], BF16, tag="bank")
+            for j in range(BIAS_TILE_HEADS):
+                c = i * BIAS_TILE_HEADS + j
                 nc.tensor.matmul(
-                    out=bias_ps[:, j * BANK : (j + 1) * BANK],
+                    out=bias_ps[:, j, :],
                     lhsT=ident_bf16[:, c : c + 1].to_broadcast([P, P]),
                     rhs=bias_rows[:],
                     start=True,
                     stop=True,
                 )
-            nc.scalar.copy(out=bias_all[:, i * BIAS_TILE : (i + 1) * BIAS_TILE], in_=bias_ps[:])
+            copy_out = nc.scalar.copy if i % 2 == 0 else nc.vector.tensor_copy
+            copy_out(
+                out=bias_all[:, i * BIAS_TILE : (i + 1) * BIAS_TILE],
+                in_=bias_ps[:].rearrange("p j n -> p (j n)"),
+            )
 
-        for i in range(BIAS_AHEAD):
+        for i in range(BIAS_TILES):
             spread_bias(i)
 
         x_pairs = x_sb[:].bitcast(F32).rearrange("r s (g p u) -> r s g p u", g=GROUPS, u=2)
@@ -194,15 +199,14 @@ def tile_selfattention_pa_kernel(tc, x, W_words, W_scales, b, out_0, out_1, out_
 
         def normalise(half, y, rsqrt):
             heads = slice(half * HALF_HEADS, (half + 1) * HALF_HEADS)
-            for kind, engine in ((0, nc.vector), (1, nc.gpsimd)):
-                inv_norm = scratch.tile([P, HALF_HEADS, SIDES], F32, name="inv_norm%d" % kind)
-                engine.tensor_scalar_min(out=inv_norm[:], in0=rsqrt[:, :, kind, :], scalar1=1.0 / EPS)
-                engine.tensor_tensor(
-                    out=y[:, heads, kind],
-                    in0=y[:, heads, kind],
-                    in1=inv_norm[:].unsqueeze(3).to_broadcast([P, HALF_HEADS, SIDES, HEAD_DIM]),
-                    op=MULT,
-                )
+            nc.vector.scalar_tensor_tensor(
+                out=y[:, heads, 0:2],
+                in0=rsqrt[:].unsqueeze(4).to_broadcast([P, HALF_HEADS, 2, SIDES, HEAD_DIM]),
+                scalar=1.0 / EPS,
+                in1=y[:, heads, 0:2],
+                op0=MIN,
+                op1=MULT,
+            )
 
         def finish(unit, half, y, rsqrt):
             normalise(half, y, rsqrt)
@@ -265,10 +269,6 @@ def tile_selfattention_pa_kernel(tc, x, W_words, W_scales, b, out_0, out_1, out_
         for unit in range(UNITS - 1):
             y = results.tile([P, UNIT_HEADS, KINDS, SIDES, HEAD_DIM], F32)
             for bank in range(UNIT_BANKS):
-                banks_done = unit * UNIT_BANKS + bank
-                next_bias = banks_done // 2 + BIAS_AHEAD
-                if banks_done % 2 == 0 and next_bias < BIAS_TILES:
-                    spread_bias(next_bias)
                 project(unit, bank, y)
                 for job in begun:
                     finish(*job)

from contextlib import ExitStack

import concourse.mybir as mybir
from concourse.masks import make_identity

F32 = mybir.dt.float32
BF16 = mybir.dt.bfloat16
I32 = mybir.dt.int32
U32 = mybir.dt.uint32
U8 = mybir.dt.uint8
FP8X4 = mybir.dt.float8_e4m3fn_x4
FP4X4 = mybir.dt.float4_e2m1fn_x4
ADD = mybir.AluOpType.add
MULT = mybir.AluOpType.mult
MIN = mybir.AluOpType.min
SQUARE = mybir.ActivationFunctionType.Square
RSQRT = mybir.ActivationFunctionType.Abs_reciprocal_sqrt

P = 128
BATCH, POSITIONS, CHANNELS, HEADS = 4, 64, 2048, 16
HEAD_DIM = CHANNELS // HEADS
KINDS = 3
COLUMNS = KINDS * CHANNELS
SIDES = 2
PAIRS = POSITIONS // SIDES
K_PASS = 4 * P
GROUPS = CHANNELS // K_PASS
BANK = 512
UNIT_HEADS = 4
UNIT = UNIT_HEADS * KINDS * HEAD_DIM
UNITS = COLUMNS // UNIT
UNIT_BANKS = UNIT // BANK
BANK_VECTORS = BANK // HEAD_DIM
HALF_HEADS = UNIT_HEADS // 2
HEAD_COLUMNS = KINDS * HEAD_DIM
BIAS_TILE_HEADS = 2
BIAS_TILE = BIAS_TILE_HEADS * HEAD_COLUMNS
BIAS_TILES = COLUMNS // BIAS_TILE
EPS = 1e-12

FLOPS = 2 * BATCH * POSITIONS * CHANNELS * COLUMNS


def tile_selfattention_pa_kernel(tc, x, W_words, W_scales, b, out_0, out_1, out_2):
    nc = tc.nc
    outs = (out_0, out_1, out_2)
    with ExitStack() as ctx:
        ctx.enter_context(tc.manual_schedule())
        keep = ctx.enter_context(tc.tile_pool(name="keep", bufs=1))
        results = ctx.enter_context(tc.tile_pool(name="results", bufs=UNITS))
        scratch = ctx.enter_context(tc.tile_pool(name="scratch", bufs=2))
        psum = ctx.enter_context(tc.psum_pool(name="psum", bufs=8))

        bias_rows = keep.tile([P, HEAD_COLUMNS], BF16)
        nc.gpsimd.memset(bias_rows[:], 0.0)
        nc.sync.dma_start(
            out=bias_rows[0:HEADS, :], in_=b.rearrange("(c n) -> c n", n=HEAD_COLUMNS)
        )

        x_sb = keep.tile([P, SIDES, CHANNELS], BF16)
        for batch in range(BATCH):
            nc.sync.dma_start(
                out=x_sb[batch:P:BATCH],
                in_=x[batch].rearrange("(pair side) e -> pair side e", side=SIDES),
            )

        words_dram = W_words.bitcast(I32)
        scales_dram = W_scales.bitcast(I32)
        w_words = []
        w_scales = []
        for unit in range(UNITS):
            plane = keep.tile([P, GROUPS, UNIT], U8, name="w_scales%d" % unit, align_bytes=64)
            nc.vector.memset(plane[:].bitcast(I32), 0)
            scale_cols = slice(unit * UNIT // 4, (unit + 1) * UNIT // 4)
            for q in range(8):
                live_row = 32 * (q // 4) + q % 4
                nc.sync.dma_start(
                    out=plane[live_row:P:64].bitcast(I32),
                    in_=scales_dram[:, q:16:8, scale_cols].rearrange("g q n -> q g n"),
                )
            words = keep.tile([P, GROUPS, 2 * UNIT], U8, name="w_words%d" % unit, align_bytes=64)
            pieces = UNIT_BANKS if unit == 0 else 1
            piece = UNIT // 2 // pieces
            for i in range(pieces):
                nc.sync.dma_start(
                    out=words[:].bitcast(I32)[:, :, i * piece : (i + 1) * piece],
                    in_=words_dram[
                        :, :, unit * UNIT // 2 + i * piece : unit * UNIT // 2 + (i + 1) * piece
                    ].rearrange("g p n -> p g n"),
                )
            w_words.append(words)
            w_scales.append(plane)

        ident_bf16 = keep.tile([P, P], BF16)
        make_identity(nc, ident_bf16[:])
        ident_f32 = keep.tile([P, P], F32)
        make_identity(nc, ident_f32[:])
        bias_all = keep.tile([P, COLUMNS], BF16)

        def spread_bias(i):
            bias_ps = psum.tile([P, BIAS_TILE_HEADS, HEAD_COLUMNS], BF16, tag="bank")
            for j in range(BIAS_TILE_HEADS):
                c = i * BIAS_TILE_HEADS + j
                nc.tensor.matmul(
                    out=bias_ps[:, j, :],
                    lhsT=ident_bf16[:, c : c + 1].to_broadcast([P, P]),
                    rhs=bias_rows[:],
                    start=True,
                    stop=True,
                )
            copy_out = nc.scalar.copy if i % 2 == 0 else nc.vector.tensor_copy
            copy_out(
                out=bias_all[:, i * BIAS_TILE : (i + 1) * BIAS_TILE],
                in_=bias_ps[:].rearrange("p j n -> p (j n)"),
            )

        for i in range(BIAS_TILES):
            spread_bias(i)

        x_pairs = x_sb[:].bitcast(F32).rearrange("r s (g p u) -> r s g p u", g=GROUPS, u=2)
        x_codes = []
        x_scales = []
        for side in range(SIDES):
            grouped = keep.tile([P, 4 * GROUPS * P], BF16, name="grouped%d" % side, align_bytes=64)
            grouped_pairs = grouped[:].bitcast(F32).rearrange("p (g r u) -> p g r u", g=GROUPS, u=2)
            for g0 in range(0, GROUPS, 2):
                xt = psum.tile([P, 2, 2, P], F32, tag="bank")
                for i in range(2):
                    for u in range(2):
                        nc.tensor.transpose(
                            xt[:, i, u, :], x_pairs[:, side, g0 + i, :, u], ident_f32[:]
                        )
                copy_out = nc.vector.tensor_copy if g0 == 0 else nc.scalar.copy
                copy_out(
                    out=grouped_pairs[:, g0 : g0 + 2], in_=xt[:].rearrange("p g u r -> p g r u")
                )
            codes = keep.tile([P, GROUPS * P], U32, name="x_codes%d" % side, align_bytes=64)
            plane = keep.tile([P, GROUPS * P], U8, name="x_scales%d" % side, align_bytes=64)
            nc.vector.quantize_mx(out=codes[:].bitcast(FP8X4), scales=plane[:], in_=grouped[:])
            x_codes.append(codes)
            x_scales.append(plane)

        def project(unit, bank, y):
            y_vectors = y[:].rearrange("p h t s d -> p (h t) s d")
            first_col = unit * UNIT + bank * BANK
            for side in range(SIDES):
                acc = psum.tile([P, BANK], F32, tag="bank")
                for g in range(GROUPS):
                    tokens = slice(g * P, (g + 1) * P)
                    nc.tensor.matmul_mx(
                        out=acc[:],
                        lhsT=x_codes[side][:, tokens].bitcast(FP8X4),
                        lhsT_scale=x_scales[side][:, tokens],
                        rhs=w_words[unit][:, g, 2 * bank * BANK : 2 * (bank + 1) * BANK].bitcast(FP4X4),
                        rhs_scale=w_scales[unit][:, g, bank * BANK : (bank + 1) * BANK],
                        start=(g == 0),
                        stop=(g == GROUPS - 1),
                    )
                nc.vector.tensor_tensor(
                    out=y_vectors[:, bank * BANK_VECTORS : (bank + 1) * BANK_VECTORS, side, :],
                    in0=acc[:].rearrange("p (v d) -> p v d", d=HEAD_DIM),
                    in1=bias_all[:, first_col : first_col + BANK].rearrange(
                        "p (v d) -> p v d", d=HEAD_DIM
                    ),
                    op=ADD,
                )

        def store_kind(unit, h_unit, heads, kind, y):
            h_all = unit * UNIT_HEADS + h_unit
            for batch in range(BATCH):
                nc.sync.dma_start(
                    out=outs[kind][batch, h_all : h_all + heads].rearrange(
                        "h (pair side) d -> pair h (side d)", side=SIDES
                    ),
                    in_=y[batch:P:BATCH, h_unit : h_unit + heads, kind].rearrange(
                        "p h s d -> p h (s d)"
                    ),
                )

        def store(unit, h_unit, heads, y):
            for kind in (2, 0, 1):
                store_kind(unit, h_unit, heads, kind, y)

        def inverse_norms(half, y):
            squares = scratch.tile([P, HALF_HEADS, 2, SIDES, HEAD_DIM], F32)
            sumsq = scratch.tile([P, HALF_HEADS, 2, SIDES], F32)
            for h in range(HALF_HEADS):
                for kind in range(2):
                    for side in range(SIDES):
                        nc.scalar.activation(
                            out=squares[:, h, kind, side, :],
                            in_=y[:, half * HALF_HEADS + h, kind, side, :],
                            func=SQUARE,
                            accum_out=sumsq[:, h, kind, side : side + 1],
                        )
            rsqrt = scratch.tile([P, HALF_HEADS, 2, SIDES], F32)
            nc.scalar.activation(out=rsqrt[:], in_=sumsq[:], func=RSQRT)
            return rsqrt

        def normalise(half, y, rsqrt):
            heads = slice(half * HALF_HEADS, (half + 1) * HALF_HEADS)
            nc.vector.scalar_tensor_tensor(
                out=y[:, heads, 0:2],
                in0=rsqrt[:].unsqueeze(4).to_broadcast([P, HALF_HEADS, 2, SIDES, HEAD_DIM]),
                scalar=1.0 / EPS,
                in1=y[:, heads, 0:2],
                op0=MIN,
                op1=MULT,
            )

        def finish(unit, half, y, rsqrt):
            normalise(half, y, rsqrt)
            if half == 1:
                store(unit, 0, UNIT_HEADS, y)

        def project_piece(unit, kind, half, y):
            heads = slice(half * HALF_HEADS, (half + 1) * HALF_HEADS)
            bias_unit = bias_all[:, unit * UNIT : (unit + 1) * UNIT].rearrange(
                "p (h t d) -> p h t d", t=KINDS, d=HEAD_DIM
            )
            for side in range(SIDES):
                acc = psum.tile([P, HALF_HEADS, HEAD_DIM], F32, tag="bank")
                for h in range(HALF_HEADS):
                    col = ((half * HALF_HEADS + h) * KINDS + kind) * HEAD_DIM
                    for g in range(GROUPS):
                        tokens = slice(g * P, (g + 1) * P)
                        nc.tensor.matmul_mx(
                            out=acc[:, h, :],
                            lhsT=x_codes[side][:, tokens].bitcast(FP8X4),
                            lhsT_scale=x_scales[side][:, tokens],
                            rhs=w_words[unit][:, g, 2 * col : 2 * (col + HEAD_DIM)].bitcast(FP4X4),
                            rhs_scale=w_scales[unit][:, g, col : col + HEAD_DIM],
                            start=(g == 0),
                            stop=(g == GROUPS - 1),
                        )
                nc.vector.tensor_tensor(
                    out=y[:, heads, kind, side, :], in0=acc[:], in1=bias_unit[:, heads, kind, :], op=ADD
                )

        def piece_norms(kind, half, y):
            squares_p = scratch.tile([P, SIDES, HALF_HEADS, HEAD_DIM], F32)
            sumsq_p = scratch.tile([P, HALF_HEADS, SIDES], F32)
            for side in range(SIDES):
                for h in range(HALF_HEADS):
                    nc.scalar.activation(
                        out=squares_p[:, side, h, :],
                        in_=y[:, half * HALF_HEADS + h, kind, side, :],
                        func=SQUARE,
                        accum_out=sumsq_p[:, h, side : side + 1],
                    )
            rsqrt_p = scratch.tile([P, HALF_HEADS, SIDES], F32)
            nc.scalar.activation(out=rsqrt_p[:], in_=sumsq_p[:], func=RSQRT)
            return rsqrt_p

        def finish_piece(unit, kind, half, y, rsqrt_p):
            heads = slice(half * HALF_HEADS, (half + 1) * HALF_HEADS)
            nc.vector.scalar_tensor_tensor(
                out=y[:, heads, kind],
                in0=rsqrt_p[:].unsqueeze(3).to_broadcast([P, HALF_HEADS, SIDES, HEAD_DIM]),
                scalar=1.0 / EPS,
                in1=y[:, heads, kind],
                op0=MIN,
                op1=MULT,
            )
            if half == 1:
                store_kind(unit, 0, UNIT_HEADS, kind, y)

        begun = []
        for unit in range(UNITS - 1):
            y = results.tile([P, UNIT_HEADS, KINDS, SIDES, HEAD_DIM], F32)
            for bank in range(UNIT_BANKS):
                project(unit, bank, y)
                for job in begun:
                    finish(*job)
                begun = []
                if bank >= 1:
                    begun = [(unit, bank - 1, y, inverse_norms(bank - 1, y))]

        unit = UNITS - 1
        y_last = results.tile([P, UNIT_HEADS, KINDS, SIDES, HEAD_DIM], F32, name="y")
        pieces_begun = []
        for kind in range(KINDS):
            for half in range(2):
                project_piece(unit, kind, half, y_last)
                for job in begun:
                    finish(*job)
                begun = []
                for job in pieces_begun:
                    finish_piece(*job)
                pieces_begun = []
                if kind < 2:
                    pieces_begun = [(unit, kind, half, y_last, piece_norms(kind, half, y_last))]
        store_kind(unit, 0, UNIT_HEADS, 2, y_last)
